import numpy as np
import ml_dtypes

BF16 = ml_dtypes.bfloat16


def bf(x):
    return np.asarray(x, np.float32).astype(BF16)


def f32(x):
    return np.asarray(x, np.float32)


def f64(x):
    return np.asarray(x).astype(np.float64)


def striped(idx):
    return np.tile(idx.reshape(-1, 16).T, (8, 1))


C, S, K, D0, D1, D2, M, N, H, R = 512, 1024, 16, 512, 512, 1024, 2048, 8192, 512, 16


def setup_inputs():
    idx = np.concatenate([np.random.permutation(S)[:H] for _ in range(R)])
    return {
        "x": f32(np.random.standard_normal((C, S))),
        "w0": f32(np.sqrt(2.0 / K) * np.random.standard_normal((1, N))),
        "b0": f32(0.1 * np.random.standard_normal((D0, 1))),
        "w1": bf(np.sqrt(2.0 / D0) * np.random.standard_normal((D0, D1))),
        "b1": f32(0.1 * np.random.standard_normal((D1, 1))),
        "w2": bf(np.sqrt(2.0 / D1) * np.random.standard_normal((D1, D2))),
        "b2": f32(0.1 * np.random.standard_normal((D2, 1))),
        "fc_w": bf(np.random.standard_normal((D2, M)) / np.sqrt(D2)),
        "fc_b": f32(0.1 * np.random.standard_normal((M, 1))),
        "offs": striped(idx),
    }


def reference(x, w0, b0, w1, b1, w2, b2, fc_w, fc_b, offs):
    idx = offs[:16].T.reshape(-1)
    p = f64(x)[:, idx] * f64(w0)
    h0 = np.maximum(p.reshape(C, D0, K).sum(axis=-1) + f64(b0).T, 0.0)
    h1 = np.maximum(h0 @ f64(w1) + f64(b1).T, 0.0)
    h2 = np.maximum(h1 @ f64(w2) + f64(b2).T, 0.0)
    return h2 @ f64(fc_w) + f64(fc_b).T

@@ -1,0 +1,130 @@
+import concourse.mybir as mybir
+from concourse.masks import make_identity
+
+F32 = mybir.dt.float32
+BF16 = mybir.dt.bfloat16
+U16 = mybir.dt.uint16
+MULT = mybir.AluOpType.mult
+ADD = mybir.AluOpType.add
+RELU = mybir.ActivationFunctionType.Relu
+
+P = 128
+C, S, K = 512, 1024, 16
+D0, D1, D2, M = 512, 512, 1024, 2048
+N = D0 * K
+PIECE = S
+BANK = 512
+
+FLOPS = 2 * C * (N + D0 * D1 + D1 * D2 + D2 * M)
+
+
+def tile_lcn_b_kernel(tc, x, w0, b0, w1, b1, w2, b2, fc_w, fc_b, offs, out):
+    nc = tc.nc
+    with (
+        tc.tile_pool(name="held", bufs=1) as held,
+        tc.tile_pool(name="products", bufs=3) as products,
+        tc.tile_pool(name="layers", bufs=2) as layers,
+        tc.tile_pool(name="results", bufs=4) as results,
+        tc.psum_pool(name="psum_layers", bufs=4) as psum_layers,
+        tc.psum_pool(name="psum_head", bufs=4) as psum_head,
+    ):
+        offsets = held.tile([P, N // 16], U16, name="offsets")
+        nc.sync.dma_start(offsets[:], offs)
+
+        x_blocks = [held.tile([P, S], F32, name="x%d" % cb) for cb in range(C // P)]
+        nc.scalar.dma_start(x_blocks[0][:], x[0:P, :])
+
+        w0_row = w0.rearrange("o n -> (o n)")
+        w0_pieces = [held.tile([P, PIECE], F32, name="w0_%d" % r) for r in range(N // PIECE)]
+        for r in range(N // PIECE):
+            nc.sync.dma_start(w0_pieces[r][:], w0_row[r * PIECE : (r + 1) * PIECE].partition_broadcast(P))
+
+        b0_cols = held.tile([P, D0 // P], F32, name="b0_cols")
+        b1_cols = held.tile([P, D1 // P], F32, name="b1_cols")
+        b2_cols = held.tile([P, D2 // P], F32, name="b2_cols")
+        with nc.allow_non_contiguous_dma(reason="a bias goes one value to a partition"):
+            nc.scalar.dma_start(b0_cols[:], b0.rearrange("(a p) o -> p (a o)", p=P))
+            nc.scalar.dma_start(b1_cols[:], b1.rearrange("(a p) o -> p (a o)", p=P))
+            nc.scalar.dma_start(b2_cols[:], b2.rearrange("(a p) o -> p (a o)", p=P))
+        for cb in range(1, C // P):
+            nc.scalar.dma_start(x_blocks[cb][:], x[cb * P : (cb + 1) * P, :])
+
+        w1_sb = held.tile([P, D0 // P, D1], BF16, name="w1_sb")
+        nc.gpsimd.dma_start(w1_sb[:], w1.rearrange("(a p) e -> p a e", p=P))
+        w2_sb = held.tile([P, D1 // P, D2], BF16, name="w2_sb")
+        nc.gpsimd.dma_start(w2_sb[:], w2.rearrange("(a p) f -> p a f", p=P))
+        fc_w_sb = held.tile([P, D2 // P, M], BF16, name="fc_w_sb")
+        nc.gpsimd.dma_start(fc_w_sb[:], fc_w.rearrange("(a p) m -> p a m", p=P))
+        fc_b_all = held.tile([P, M], F32, name="fc_b_all")
+        nc.gpsimd.dma_start(fc_b_all[:], fc_b.rearrange("m o -> (m o)").partition_broadcast(P))
+
+        identity = held.tile([P, P], F32, name="identity")
+        make_identity(nc, identity[:])
+
+        for cb in range(C // P):
+            h0_sums = layers.tile([P, D0], F32, name="h0_sums")
+            nodes = PIECE // K
+            for r in range(N // PIECE):
+                product = products.tile([P, PIECE], F32, name="product")
+                nc.vector.tensor_tensor(
+                    product[:],
+                    x_blocks[cb][:].indirect(offsets[:, r * (PIECE // 16) : (r + 1) * (PIECE // 16)]),
+                    w0_pieces[r][:],
+                    MULT,
+                )
+                nc.vector.tensor_reduce(
+                    out=h0_sums[:, r * nodes : (r + 1) * nodes],
+                    in_=product[:].rearrange("p (d k) -> p d k", k=K),
+                    axis=mybir.AxisListType.X,
+                    op=ADD,
+                )
+
+            h0_ps = psum_layers.tile([P, D0 // P, P], F32, name="h0_ps", tag="layer_ps")
+            h0 = layers.tile([P, D0 // P, P], BF16, name="h0")
+            for a in range(D0 // P):
+                nc.tensor.transpose(h0_ps[:, a, :], h0_sums[:, a * P : (a + 1) * P], identity[:])
+                nc.scalar.activation(h0[:, a, :], h0_ps[:, a, :], RELU, bias=b0_cols[:, a : a + 1])
+
+            h1_ps = psum_layers.tile([P, D1 // P, P], F32, name="h1_ps", tag="layer_ps")
+            h1 = layers.tile([P, D1 // P, P], BF16, name="h1")
+            for e in range(D1 // P):
+                for a in range(D0 // P):
+                    nc.tensor.matmul(
+                        h1_ps[:, e, :],
+                        w1_sb[:, a, e * P : (e + 1) * P],
+                        h0[:, a, :],
+                        start=(a == 0),
+                        stop=(a == D0 // P - 1),
+                    )
+                nc.scalar.activation(h1[:, e, :], h1_ps[:, e, :], RELU, bias=b1_cols[:, e : e + 1])
+
+            h2 = layers.tile([P, D2 // P, P], BF16, name="h2")
+            per_bank = BANK // P
+            for half in range(D2 // P // per_bank):
+                h2_ps = psum_layers.tile([P, per_bank, P], F32, name="h2_ps", tag="layer_ps")
+                for g in range(per_bank):
+                    f = half * per_bank + g
+                    for e in range(D1 // P):
+                        nc.tensor.matmul(
+                            h2_ps[:, g, :],
+                            w2_sb[:, e, f * P : (f + 1) * P],
+                            h1[:, e, :],
+                            start=(e == 0),
+                            stop=(e == D1 // P - 1),
+                        )
+                    nc.scalar.activation(h2[:, f, :], h2_ps[:, g, :], RELU, bias=b2_cols[:, f : f + 1])
+
+            for mc in range(M // BANK):
+                cols = slice(mc * BANK, (mc + 1) * BANK)
+                head_ps = psum_head.tile([P, BANK], F32, name="head_ps")
+                for f in range(D2 // P):
+                    nc.tensor.matmul(
+                        head_ps[:],
+                        h2[:, f, :],
+                        fc_w_sb[:, f, cols],
+                        start=(f == 0),
+                        stop=(f == D2 // P - 1),
+                    )
+                result = results.tile([P, BANK], F32, name="result")
+                nc.vector.tensor_tensor(result[:], head_ps[:], fc_b_all[:, cols], ADD)
+                nc.sync.dma_start(out[cb * P : (cb + 1) * P, cols], result[:])

@@ -5,7 +5,6 @@ F32 = mybir.dt.float32
 BF16 = mybir.dt.bfloat16
 U16 = mybir.dt.uint16
 MULT = mybir.AluOpType.mult
-ADD = mybir.AluOpType.add
 RELU = mybir.ActivationFunctionType.Relu
 
 P = 128
@@ -15,6 +14,14 @@ N = D0 * K
 PIECE = S
 BANK = 512
 
+W0_ROW = 0
+B0_ROW = W0_ROW + N // P
+B1_ROW = B0_ROW + D0 // P
+B2_ROW = B1_ROW + D1 // P
+FC_B_ROW = B2_ROW + D2 // P
+ROWS_USED = FC_B_ROW + M // P
+assert ROWS_USED == 96
+
 FLOPS = 2 * C * (N + D0 * D1 + D1 * D2 + D2 * M)
 
 
@@ -22,109 +29,138 @@ def tile_lcn_b_kernel(tc, x, w0, b0, w1, b1, w2, b2, fc_w, fc_b, offs, out):
     nc = tc.nc
     with (
         tc.tile_pool(name="held", bufs=1) as held,
-        tc.tile_pool(name="products", bufs=3) as products,
+        tc.tile_pool(name="products", bufs=4) as products,
         tc.tile_pool(name="layers", bufs=2) as layers,
         tc.tile_pool(name="results", bufs=4) as results,
-        tc.psum_pool(name="psum_layers", bufs=4) as psum_layers,
-        tc.psum_pool(name="psum_head", bufs=4) as psum_head,
+        tc.psum_pool(name="psum_sums", bufs=1) as psum_sums,
+        tc.psum_pool(name="psum_hidden", bufs=3) as psum_hidden,
+        tc.psum_pool(name="psum_wide", bufs=4) as psum_wide,
     ):
-        offsets = held.tile([P, N // 16], U16, name="offsets")
-        nc.sync.dma_start(offsets[:], offs)
-
-        x_blocks = [held.tile([P, S], F32, name="x%d" % cb) for cb in range(C // P)]
-        nc.scalar.dma_start(x_blocks[0][:], x[0:P, :])
-
-        w0_row = w0.rearrange("o n -> (o n)")
-        w0_pieces = [held.tile([P, PIECE], F32, name="w0_%d" % r) for r in range(N // PIECE)]
-        for r in range(N // PIECE):
-            nc.sync.dma_start(w0_pieces[r][:], w0_row[r * PIECE : (r + 1) * PIECE].partition_broadcast(P))
-
-        b0_cols = held.tile([P, D0 // P], F32, name="b0_cols")
-        b1_cols = held.tile([P, D1 // P], F32, name="b1_cols")
-        b2_cols = held.tile([P, D2 // P], F32, name="b2_cols")
-        with nc.allow_non_contiguous_dma(reason="a bias goes one value to a partition"):
-            nc.scalar.dma_start(b0_cols[:], b0.rearrange("(a p) o -> p (a o)", p=P))
-            nc.scalar.dma_start(b1_cols[:], b1.rearrange("(a p) o -> p (a o)", p=P))
-            nc.scalar.dma_start(b2_cols[:], b2.rearrange("(a p) o -> p (a o)", p=P))
-        for cb in range(1, C // P):
-            nc.scalar.dma_start(x_blocks[cb][:], x[cb * P : (cb + 1) * P, :])
-
-        w1_sb = held.tile([P, D0 // P, D1], BF16, name="w1_sb")
-        nc.gpsimd.dma_start(w1_sb[:], w1.rearrange("(a p) e -> p a e", p=P))
-        w2_sb = held.tile([P, D1 // P, D2], BF16, name="w2_sb")
-        nc.gpsimd.dma_start(w2_sb[:], w2.rearrange("(a p) f -> p a f", p=P))
-        fc_w_sb = held.tile([P, D2 // P, M], BF16, name="fc_w_sb")
-        nc.gpsimd.dma_start(fc_w_sb[:], fc_w.rearrange("(a p) m -> p a m", p=P))
-        fc_b_all = held.tile([P, M], F32, name="fc_b_all")
-        nc.gpsimd.dma_start(fc_b_all[:], fc_b.rearrange("m o -> (m o)").partition_broadcast(P))
-
         identity = held.tile([P, P], F32, name="identity")
         make_identity(nc, identity[:])
 
-        for cb in range(C // P):
-            h0_sums = layers.tile([P, D0], F32, name="h0_sums")
-            nodes = PIECE // K
-            for r in range(N // PIECE):
-                product = products.tile([P, PIECE], F32, name="product")
+        offsets = held.tile([P, N // 16], U16, name="offsets")
+        nc.sync.dma_start(offsets[:], offs)
+        vector_rows = held.tile([P, P], F32, name="vector_rows")
+        nc.vector.memset(vector_rows[ROWS_USED:P, :], 0.0)
+        nc.scalar.dma_start(vector_rows[W0_ROW:B0_ROW, :], w0.rearrange("o (a p) -> (o a) p", p=P))
+        nc.scalar.dma_start(vector_rows[B0_ROW:B1_ROW, :], b0.rearrange("(a p) o -> a (p o)", p=P))
+        nc.scalar.dma_start(vector_rows[B1_ROW:B2_ROW, :], b1.rearrange("(a p) o -> a (p o)", p=P))
+        nc.sync.dma_start(vector_rows[B2_ROW:FC_B_ROW, :], b2.rearrange("(a p) o -> a (p o)", p=P))
+        nc.sync.dma_start(vector_rows[FC_B_ROW:ROWS_USED, :], fc_b.rearrange("(a p) o -> a (p o)", p=P))
+        x_blocks = [held.tile([P, S], F32, name="x%d" % cb) for cb in range(C // P)]
+        nc.scalar.dma_start(x_blocks[0][:], x[0:P, :])
+
+        w1_sb = held.tile([P, D0 // P, D1], BF16, name="w1_sb")
+        nc.scalar.dma_start(w1_sb[:], w1.rearrange("(a p) e -> p a e", p=P))
+        w2_sb = held.tile([P, D1 // P, D2], BF16, name="w2_sb")
+        nc.scalar.dma_start(w2_sb[:], w2.rearrange("(a p) f -> p a f", p=P))
+        fc_w_sb = held.tile([P, D2 // P, M], BF16, name="fc_w_sb")
+        nc.sync.dma_start(fc_w_sb[:], fc_w.rearrange("(a p) m -> p a m", p=P))
+        for cb in range(1, C // P):
+            nc.scalar.dma_start(x_blocks[cb][:], x[cb * P : (cb + 1) * P, :])
+
+        vector_cols_ps = psum_wide.tile([P, BANK], F32, name="vector_cols_ps", tag="wide_ps")
+        nc.tensor.transpose(vector_cols_ps[:, 0:P], vector_rows[:], identity[:])
+        vector_cols = held.tile([P, P], F32, name="vector_cols")
+        nc.scalar.copy(vector_cols[:], vector_cols_ps[:, 0:P])
+
+        def spread(wide_ps, first, stop):
+            for g in range(BANK // P):
+                nc.tensor.matmul(
+                    wide_ps[:, g * P : (g + 1) * P],
+                    vector_cols[:, first + g : first + g + 1].to_broadcast([P, P]),
+                    identity[:],
+                    is_transpose=True,
+                    start=(g == 0),
+                    stop=(stop and g == BANK // P - 1),
+                )
+
+        w0_pieces = [held.tile([P, PIECE], F32, name="w0_%d" % r) for r in range(N // PIECE)]
+        for r in range(N // PIECE):
+            for half in range(PIECE // BANK):
+                w0_ps = psum_wide.tile([P, BANK], F32, name="w0_ps", tag="wide_ps")
+                spread(w0_ps, W0_ROW + (r * PIECE + half * BANK) // P, True)
+                if r == 0:
+                    nc.vector.tensor_copy(w0_pieces[r][:, half * BANK : (half + 1) * BANK], w0_ps[:])
+                else:
+                    nc.scalar.copy(w0_pieces[r][:, half * BANK : (half + 1) * BANK], w0_ps[:])
+
+        def look_up(cb, a):
+            product = products.tile([P, P * K], F32, name="product")
+            for half in range(P * K // PIECE):
+                r = a * (P * K // PIECE) + half
                 nc.vector.tensor_tensor(
-                    product[:],
+                    product[:, half * PIECE : (half + 1) * PIECE],
                     x_blocks[cb][:].indirect(offsets[:, r * (PIECE // 16) : (r + 1) * (PIECE // 16)]),
                     w0_pieces[r][:],
                     MULT,
                 )
-                nc.vector.tensor_reduce(
-                    out=h0_sums[:, r * nodes : (r + 1) * nodes],
-                    in_=product[:].rearrange("p (d k) -> p d k", k=K),
-                    axis=mybir.AxisListType.X,
-                    op=ADD,
-                )
+            return product
 
-            h0_ps = psum_layers.tile([P, D0 // P, P], F32, name="h0_ps", tag="layer_ps")
+        def sum_neighbours(a, product, h0_ps, h0):
+            by_neighbour = product[:].rearrange("p (d k) -> p d k", k=K)
+            for k in range(K):
+                nc.tensor.matmul(
+                    h0_ps[:, a, :],
+                    by_neighbour[:, :, k],
+                    identity[:],
+                    is_transpose=True,
+                    start=(k == 0),
+                    stop=(k == K - 1),
+                )
+            nc.scalar.activation(h0[:, a, :], h0_ps[:, a, :], RELU, bias=vector_cols[:, B0_ROW + a : B0_ROW + a + 1])
+
+        def hidden_layer(h_in, w_sb, b_row, h_out):
+            blocks_in, blocks_out = h_in.shape[1], h_out.shape[1]
+            for g in range(blocks_out):
+                hidden_ps = psum_hidden.tile([P, P], F32, name="hidden_ps")
+                for a in range(blocks_in):
+                    nc.tensor.matmul(
+                        hidden_ps[:],
+                        w_sb[:, a, g * P : (g + 1) * P],
+                        h_in[:, a, :],
+                        start=(a == 0),
+                        stop=(a == blocks_in - 1),
+                    )
+                nc.scalar.activation(h_out[:, g, :], hidden_ps[:], RELU, bias=vector_cols[:, b_row + g : b_row + g + 1])
+
+        def open_head():
+            head_banks = []
+            for mc in range(M // BANK):
+                head_ps = psum_wide.tile([P, BANK], F32, name="head_ps", tag="wide_ps")
+                spread(head_ps, FC_B_ROW + mc * (BANK // P), False)
+                head_banks.append(head_ps)
+            return head_banks
+
+        def head(cb, h2, head_ps, mc):
+            for f in range(D2 // P):
+                nc.tensor.matmul(
+                    head_ps[:],
+                    h2[:, f, :],
+                    fc_w_sb[:, f, mc * BANK : (mc + 1) * BANK],
+                    start=False,
+                    stop=(f == D2 // P - 1),
+                )
+            result = results.tile([P, BANK], F32, name="result")
+            nc.scalar.copy(result[:], head_ps[:])
+            nc.sync.dma_start(out[cb * P : (cb + 1) * P, mc * BANK : (mc + 1) * BANK], result[:])
+
+        assert M // BANK == D0 // P
+        h2_before, banks_before = None, None
+        for cb in range(C // P):
+            h0_ps = psum_sums.tile([P, D0 // P, P], F32, name="h0_ps")
             h0 = layers.tile([P, D0 // P, P], BF16, name="h0")
             for a in range(D0 // P):
-                nc.tensor.transpose(h0_ps[:, a, :], h0_sums[:, a * P : (a + 1) * P], identity[:])
-                nc.scalar.activation(h0[:, a, :], h0_ps[:, a, :], RELU, bias=b0_cols[:, a : a + 1])
-
-            h1_ps = psum_layers.tile([P, D1 // P, P], F32, name="h1_ps", tag="layer_ps")
+                product = look_up(cb, a)
+                if cb > 0:
+                    head(cb - 1, h2_before, banks_before[a], a)
+                sum_neighbours(a, product, h0_ps, h0)
+            banks_before = open_head()
             h1 = layers.tile([P, D1 // P, P], BF16, name="h1")
-            for e in range(D1 // P):
-                for a in range(D0 // P):
-                    nc.tensor.matmul(
-                        h1_ps[:, e, :],
-                        w1_sb[:, a, e * P : (e + 1) * P],
-                        h0[:, a, :],
-                        start=(a == 0),
-                        stop=(a == D0 // P - 1),
-                    )
-                nc.scalar.activation(h1[:, e, :], h1_ps[:, e, :], RELU, bias=b1_cols[:, e : e + 1])
-
             h2 = layers.tile([P, D2 // P, P], BF16, name="h2")
-            per_bank = BANK // P
-            for half in range(D2 // P // per_bank):
-                h2_ps = psum_layers.tile([P, per_bank, P], F32, name="h2_ps", tag="layer_ps")
-                for g in range(per_bank):
-                    f = half * per_bank + g
-                    for e in range(D1 // P):
-                        nc.tensor.matmul(
-                            h2_ps[:, g, :],
-                            w2_sb[:, e, f * P : (f + 1) * P],
-                            h1[:, e, :],
-                            start=(e == 0),
-                            stop=(e == D1 // P - 1),
-                        )
-                    nc.scalar.activation(h2[:, f, :], h2_ps[:, g, :], RELU, bias=b2_cols[:, f : f + 1])
-
-            for mc in range(M // BANK):
-                cols = slice(mc * BANK, (mc + 1) * BANK)
-                head_ps = psum_head.tile([P, BANK], F32, name="head_ps")
-                for f in range(D2 // P):
-                    nc.tensor.matmul(
-                        head_ps[:],
-                        h2[:, f, :],
-                        fc_w_sb[:, f, cols],
-                        start=(f == 0),
-                        stop=(f == D2 // P - 1),
-                    )
-                result = results.tile([P, BANK], F32, name="result")
-                nc.vector.tensor_tensor(result[:], head_ps[:], fc_b_all[:, cols], ADD)
-                nc.sync.dma_start(out[cb * P : (cb + 1) * P, cols], result[:])
+            hidden_layer(h0, w1_sb, B1_ROW, h1)
+            hidden_layer(h1, w2_sb, B2_ROW, h2)
+            h2_before = h2
+        for mc in range(M // BANK):
+            head(C // P - 1, h2_before, banks_before[mc], mc)

@@ -5,6 +5,7 @@ F32 = mybir.dt.float32
 BF16 = mybir.dt.bfloat16
 U16 = mybir.dt.uint16
 MULT = mybir.AluOpType.mult
+ADD = mybir.AluOpType.add
 RELU = mybir.ActivationFunctionType.Relu
 
 P = 128
@@ -14,13 +15,10 @@ N = D0 * K
 PIECE = S
 BANK = 512
 
-W0_ROW = 0
-B0_ROW = W0_ROW + N // P
+B0_ROW = 0
 B1_ROW = B0_ROW + D0 // P
 B2_ROW = B1_ROW + D1 // P
-FC_B_ROW = B2_ROW + D2 // P
-ROWS_USED = FC_B_ROW + M // P
-assert ROWS_USED == 96
+ROWS_USED = B2_ROW + D2 // P
 
 FLOPS = 2 * C * (N + D0 * D1 + D1 * D2 + D2 * M)
 
@@ -31,60 +29,51 @@ def tile_lcn_b_kernel(tc, x, w0, b0, w1, b1, w2, b2, fc_w, fc_b, offs, out):
         tc.tile_pool(name="held", bufs=1) as held,
         tc.tile_pool(name="products", bufs=4) as products,
         tc.tile_pool(name="layers", bufs=2) as layers,
-        tc.tile_pool(name="results", bufs=4) as results,
+        tc.tile_pool(name="results", bufs=C // P * (M // BANK)) as results,
         tc.psum_pool(name="psum_sums", bufs=1) as psum_sums,
-        tc.psum_pool(name="psum_hidden", bufs=3) as psum_hidden,
-        tc.psum_pool(name="psum_wide", bufs=4) as psum_wide,
+        tc.psum_pool(name="psum_hidden", bufs=5) as psum_hidden,
+        tc.psum_pool(name="psum_wide", bufs=2) as psum_wide,
     ):
         identity = held.tile([P, P], F32, name="identity")
         make_identity(nc, identity[:])
 
         offsets = held.tile([P, N // 16], U16, name="offsets")
         nc.sync.dma_start(offsets[:], offs)
-        vector_rows = held.tile([P, P], F32, name="vector_rows")
-        nc.vector.memset(vector_rows[ROWS_USED:P, :], 0.0)
-        nc.scalar.dma_start(vector_rows[W0_ROW:B0_ROW, :], w0.rearrange("o (a p) -> (o a) p", p=P))
-        nc.scalar.dma_start(vector_rows[B0_ROW:B1_ROW, :], b0.rearrange("(a p) o -> a (p o)", p=P))
-        nc.scalar.dma_start(vector_rows[B1_ROW:B2_ROW, :], b1.rearrange("(a p) o -> a (p o)", p=P))
-        nc.sync.dma_start(vector_rows[B2_ROW:FC_B_ROW, :], b2.rearrange("(a p) o -> a (p o)", p=P))
-        nc.sync.dma_start(vector_rows[FC_B_ROW:ROWS_USED, :], fc_b.rearrange("(a p) o -> a (p o)", p=P))
         x_blocks = [held.tile([P, S], F32, name="x%d" % cb) for cb in range(C // P)]
         nc.scalar.dma_start(x_blocks[0][:], x[0:P, :])
+        bias_rows = held.tile([P, P], F32, name="bias_rows")
+        nc.vector.memset(bias_rows[:], 0.0)
+        nc.scalar.dma_start(bias_rows[B0_ROW:B1_ROW, :], b0.rearrange("(a p) o -> a (p o)", p=P))
+        nc.scalar.dma_start(bias_rows[B1_ROW:B2_ROW, :], b1.rearrange("(a p) o -> a (p o)", p=P))
+        nc.scalar.dma_start(bias_rows[B2_ROW:ROWS_USED, :], b2.rearrange("(a p) o -> a (p o)", p=P))
 
-        w1_sb = held.tile([P, D0 // P, D1], BF16, name="w1_sb")
-        nc.scalar.dma_start(w1_sb[:], w1.rearrange("(a p) e -> p a e", p=P))
-        w2_sb = held.tile([P, D1 // P, D2], BF16, name="w2_sb")
-        nc.scalar.dma_start(w2_sb[:], w2.rearrange("(a p) f -> p a f", p=P))
-        fc_w_sb = held.tile([P, D2 // P, M], BF16, name="fc_w_sb")
-        nc.sync.dma_start(fc_w_sb[:], fc_w.rearrange("(a p) m -> p a m", p=P))
-        for cb in range(1, C // P):
-            nc.scalar.dma_start(x_blocks[cb][:], x[cb * P : (cb + 1) * P, :])
-
-        vector_cols_ps = psum_wide.tile([P, BANK], F32, name="vector_cols_ps", tag="wide_ps")
-        nc.tensor.transpose(vector_cols_ps[:, 0:P], vector_rows[:], identity[:])
-        vector_cols = held.tile([P, P], F32, name="vector_cols")
-        nc.scalar.copy(vector_cols[:], vector_cols_ps[:, 0:P])
-
-        def spread(wide_ps, first, stop):
-            for g in range(BANK // P):
-                nc.tensor.matmul(
-                    wide_ps[:, g * P : (g + 1) * P],
-                    vector_cols[:, first + g : first + g + 1].to_broadcast([P, P]),
-                    identity[:],
-                    is_transpose=True,
-                    start=(g == 0),
-                    stop=(stop and g == BANK // P - 1),
-                )
-
+        w0_row = w0.rearrange("o n -> (o n)")
         w0_pieces = [held.tile([P, PIECE], F32, name="w0_%d" % r) for r in range(N // PIECE)]
         for r in range(N // PIECE):
-            for half in range(PIECE // BANK):
-                w0_ps = psum_wide.tile([P, BANK], F32, name="w0_ps", tag="wide_ps")
-                spread(w0_ps, W0_ROW + (r * PIECE + half * BANK) // P, True)
-                if r == 0:
-                    nc.vector.tensor_copy(w0_pieces[r][:, half * BANK : (half + 1) * BANK], w0_ps[:])
-                else:
-                    nc.scalar.copy(w0_pieces[r][:, half * BANK : (half + 1) * BANK], w0_ps[:])
+            nc.sync.dma_start(w0_pieces[r][:], w0_row[r * PIECE : (r + 1) * PIECE].partition_broadcast(P))
+        nc.sync.dma_start(x_blocks[1][:], x[P : 2 * P, :])
+
+        w1_sb = held.tile([P, D0 // P, D1], BF16, name="w1_sb")
+        nc.sync.dma_start(w1_sb[:], w1.rearrange("(a p) e -> p a e", p=P))
+        w2_sb = held.tile([P, D1 // P, D2], BF16, name="w2_sb")
+        nc.sync.dma_start(w2_sb[:], w2.rearrange("(a p) f -> p a f", p=P))
+        fc_w_blocks = fc_w.rearrange("(a p) m -> p a m", p=P)
+        fc_w_sb = [held.tile([P, D2 // P, BANK], BF16, name="fc_w_%d" % mc) for mc in range(M // BANK)]
+        for mc in range(M // BANK):
+            nc.sync.dma_start(fc_w_sb[mc][:], fc_w_blocks[:, :, mc * BANK : (mc + 1) * BANK])
+        for cb in range(2, C // P):
+            nc.sync.dma_start(x_blocks[cb][:], x[cb * P : (cb + 1) * P, :])
+        fc_b_row = fc_b.rearrange("m o -> (m o)")
+        fc_b_pieces = []
+        for i in range(M // PIECE):
+            fc_b_piece = held.tile([P, PIECE], F32, name="fc_b_%d" % i, tag="w0_%d" % (N // PIECE - M // PIECE + i))
+            nc.sync.dma_start(fc_b_piece[:], fc_b_row[i * PIECE : (i + 1) * PIECE].partition_broadcast(P))
+            fc_b_pieces.append(fc_b_piece)
+
+        bias_cols_ps = psum_wide.tile([P, BANK], F32, name="bias_cols_ps", tag="head_ps")
+        nc.tensor.transpose(bias_cols_ps[:, 0:P], bias_rows[:], identity[:])
+        bias_cols = held.tile([P, P], F32, name="bias_cols")
+        nc.scalar.copy(bias_cols[:], bias_cols_ps[:, 0:P])
 
         def look_up(cb, a):
             product = products.tile([P, P * K], F32, name="product")
@@ -109,7 +98,7 @@ def tile_lcn_b_kernel(tc, x, w0, b0, w1, b1, w2, b2, fc_w, fc_b, offs, out):
                     start=(k == 0),
                     stop=(k == K - 1),
                 )
-            nc.scalar.activation(h0[:, a, :], h0_ps[:, a, :], RELU, bias=vector_cols[:, B0_ROW + a : B0_ROW + a + 1])
+            nc.scalar.activation(h0[:, a, :], h0_ps[:, a, :], RELU, bias=bias_cols[:, B0_ROW + a : B0_ROW + a + 1])
 
         def hidden_layer(h_in, w_sb, b_row, h_out):
             blocks_in, blocks_out = h_in.shape[1], h_out.shape[1]
@@ -123,44 +112,57 @@ def tile_lcn_b_kernel(tc, x, w0, b0, w1, b1, w2, b2, fc_w, fc_b, offs, out):
                         start=(a == 0),
                         stop=(a == blocks_in - 1),
                     )
-                nc.scalar.activation(h_out[:, g, :], hidden_ps[:], RELU, bias=vector_cols[:, b_row + g : b_row + g + 1])
+                nc.scalar.activation(h_out[:, g, :], hidden_ps[:], RELU, bias=bias_cols[:, b_row + g : b_row + g + 1])
 
-        def open_head():
-            head_banks = []
-            for mc in range(M // BANK):
-                head_ps = psum_wide.tile([P, BANK], F32, name="head_ps", tag="wide_ps")
-                spread(head_ps, FC_B_ROW + mc * (BANK // P), False)
-                head_banks.append(head_ps)
-            return head_banks
-
-        def head(cb, h2, head_ps, mc):
-            for f in range(D2 // P):
+        def head(head_ps, h2, mc, blocks):
+            for f in blocks:
                 nc.tensor.matmul(
                     head_ps[:],
                     h2[:, f, :],
-                    fc_w_sb[:, f, mc * BANK : (mc + 1) * BANK],
-                    start=False,
+                    fc_w_sb[mc][:, f, :],
+                    start=(f == 0),
                     stop=(f == D2 // P - 1),
                 )
-            result = results.tile([P, BANK], F32, name="result")
-            nc.scalar.copy(result[:], head_ps[:])
+
+        def add_bias_and_store(cb, mc, product_with_fc_w, result):
+            first = mc * BANK % PIECE
+            fc_b_part = fc_b_pieces[mc * BANK // PIECE][:, first : first + BANK]
+            nc.vector.tensor_tensor(result[:], product_with_fc_w[:], fc_b_part, ADD)
             nc.sync.dma_start(out[cb * P : (cb + 1) * P, mc * BANK : (mc + 1) * BANK], result[:])
 
-        assert M // BANK == D0 // P
-        h2_before, banks_before = None, None
+        parked = []
+
+        def park(cb, mc, head_ps):
+            result = results.tile([P, BANK], F32, name="result")
+            nc.scalar.copy(result[:], head_ps[:])
+            parked.append((cb, mc, result))
+
+        quarters = M // BANK
+        assert quarters == D0 // P
+        all_blocks = range(D2 // P)
+        first_half, second_half = range(D2 // P // 2), range(D2 // P // 2, D2 // P)
+        h2_before = None
         for cb in range(C // P):
             h0_ps = psum_sums.tile([P, D0 // P, P], F32, name="h0_ps")
             h0 = layers.tile([P, D0 // P, P], BF16, name="h0")
+            h1 = layers.tile([P, D1 // P, P], BF16, name="h1")
+            h2 = layers.tile([P, D2 // P, P], BF16, name="h2")
             for a in range(D0 // P):
                 product = look_up(cb, a)
                 if cb > 0:
-                    head(cb - 1, h2_before, banks_before[a], a)
+                    head_ps = psum_wide.tile([P, BANK], F32, name="head_ps")
+                    head(head_ps, h2_before, a, first_half)
                 sum_neighbours(a, product, h0_ps, h0)
-            banks_before = open_head()
-            h1 = layers.tile([P, D1 // P, P], BF16, name="h1")
-            h2 = layers.tile([P, D2 // P, P], BF16, name="h2")
+                if cb > 0:
+                    head(head_ps, h2_before, a, second_half)
+                    park(cb - 1, a, head_ps)
             hidden_layer(h0, w1_sb, B1_ROW, h1)
             hidden_layer(h1, w2_sb, B2_ROW, h2)
             h2_before = h2
-        for mc in range(M // BANK):
-            head(C // P - 1, h2_before, banks_before[mc], mc)
+        for cb, mc, result in parked:
+            add_bias_and_store(cb, mc, result, result)
+        for mc in range(quarters):
+            head_ps = psum_wide.tile([P, BANK], F32, name="head_ps")
+            head(head_ps, h2_before, mc, all_blocks)
+            result = results.tile([P, BANK], F32, name="result")
+            add_bias_and_store(C // P - 1, mc, head_ps, result)

@@ -28,6 +28,7 @@ def tile_lcn_b_kernel(tc, x, w0, b0, w1, b1, w2, b2, fc_w, fc_b, offs, out):
     with (
         tc.tile_pool(name="held", bufs=1) as held,
         tc.tile_pool(name="products", bufs=4) as products,
+        tc.tile_pool(name="folded_products", bufs=2) as folded_products,
         tc.tile_pool(name="layers", bufs=2) as layers,
         tc.tile_pool(name="results", bufs=C // P * (M // BANK)) as results,
         tc.psum_pool(name="psum_sums", bufs=1) as psum_sums,
@@ -87,16 +88,24 @@ def tile_lcn_b_kernel(tc, x, w0, b0, w1, b1, w2, b2, fc_w, fc_b, offs, out):
                 )
             return product
 
-        def sum_neighbours(a, product, h0_ps, h0):
-            by_neighbour = product[:].rearrange("p (d k) -> p d k", k=K)
-            for k in range(K):
+        def fold(product):
+            halves = product[:].rearrange("p (d h k) -> p d h k", h=2, k=K // 2)
+            folded = folded_products.tile([P, P * K // 2], F32, name="folded")
+            nc.vector.tensor_tensor(
+                folded[:].rearrange("p (d k) -> p d k", k=K // 2), halves[:, :, 0, :], halves[:, :, 1, :], ADD
+            )
+            return folded
+
+        def sum_neighbours(a, terms, terms_a_node, h0_ps, h0):
+            by_term = terms[:].rearrange("p (d k) -> p d k", k=terms_a_node)
+            for k in range(terms_a_node):
                 nc.tensor.matmul(
                     h0_ps[:, a, :],
-                    by_neighbour[:, :, k],
+                    by_term[:, :, k],
                     identity[:],
                     is_transpose=True,
                     start=(k == 0),
-                    stop=(k == K - 1),
+                    stop=(k == terms_a_node - 1),
                 )
             nc.scalar.activation(h0[:, a, :], h0_ps[:, a, :], RELU, bias=bias_cols[:, B0_ROW + a : B0_ROW + a + 1])
 
@@ -152,7 +161,10 @@ def tile_lcn_b_kernel(tc, x, w0, b0, w1, b1, w2, b2, fc_w, fc_b, offs, out):
                 if cb > 0:
                     head_ps = psum_wide.tile([P, BANK], F32, name="head_ps")
                     head(head_ps, h2_before, a, first_half)
-                sum_neighbours(a, product, h0_ps, h0)
+                if cb == C // P - 1 and a >= D0 // P // 2:
+                    sum_neighbours(a, fold(product), K // 2, h0_ps, h0)
+                else:
+                    sum_neighbours(a, product, K, h0_ps, h0)
                 if cb > 0:
                     head(head_ps, h2_before, a, second_half)
                     park(cb - 1, a, head_ps)

@@ -28,7 +28,6 @@ def tile_lcn_b_kernel(tc, x, w0, b0, w1, b1, w2, b2, fc_w, fc_b, offs, out):
     with (
         tc.tile_pool(name="held", bufs=1) as held,
         tc.tile_pool(name="products", bufs=4) as products,
-        tc.tile_pool(name="folded_products", bufs=2) as folded_products,
         tc.tile_pool(name="layers", bufs=2) as layers,
         tc.tile_pool(name="results", bufs=C // P * (M // BANK)) as results,
         tc.psum_pool(name="psum_sums", bufs=1) as psum_sums,
@@ -88,26 +87,17 @@ def tile_lcn_b_kernel(tc, x, w0, b0, w1, b1, w2, b2, fc_w, fc_b, offs, out):
                 )
             return product
 
-        def fold(product):
-            halves = product[:].rearrange("p (d h k) -> p d h k", h=2, k=K // 2)
-            folded = folded_products.tile([P, P * K // 2], F32, name="folded")
-            nc.vector.tensor_tensor(
-                folded[:].rearrange("p (d k) -> p d k", k=K // 2), halves[:, :, 0, :], halves[:, :, 1, :], ADD
-            )
-            return folded
-
-        def sum_neighbours(a, terms, terms_a_node, h0_ps, h0):
-            by_term = terms[:].rearrange("p (d k) -> p d k", k=terms_a_node)
-            for k in range(terms_a_node):
+        def sum_neighbours(a, product, terms, h0_ps):
+            by_term = product[:].rearrange("p (d k) -> p d k", k=K)
+            for k in terms:
                 nc.tensor.matmul(
                     h0_ps[:, a, :],
                     by_term[:, :, k],
                     identity[:],
                     is_transpose=True,
                     start=(k == 0),
-                    stop=(k == terms_a_node - 1),
+                    stop=(k == K - 1),
                 )
-            nc.scalar.activation(h0[:, a, :], h0_ps[:, a, :], RELU, bias=bias_cols[:, B0_ROW + a : B0_ROW + a + 1])
 
         def hidden_layer(h_in, w_sb, b_row, h_out):
             blocks_in, blocks_out = h_in.shape[1], h_out.shape[1]
@@ -150,6 +140,8 @@ def tile_lcn_b_kernel(tc, x, w0, b0, w1, b1, w2, b2, fc_w, fc_b, offs, out):
         assert quarters == D0 // P
         all_blocks = range(D2 // P)
         first_half, second_half = range(D2 // P // 2), range(D2 // P // 2, D2 // P)
+        third_quarter, fourth_quarter = range(D2 // P // 2, D2 // P * 3 // 4), range(D2 // P * 3 // 4, D2 // P)
+        first_terms, last_terms = range(K // 2), range(K // 2, K)
         h2_before = None
         for cb in range(C // P):
             h0_ps = psum_sums.tile([P, D0 // P, P], F32, name="h0_ps")
@@ -161,13 +153,17 @@ def tile_lcn_b_kernel(tc, x, w0, b0, w1, b1, w2, b2, fc_w, fc_b, offs, out):
                 if cb > 0:
                     head_ps = psum_wide.tile([P, BANK], F32, name="head_ps")
                     head(head_ps, h2_before, a, first_half)
-                if cb == C // P - 1 and a >= D0 // P // 2:
-                    sum_neighbours(a, fold(product), K // 2, h0_ps, h0)
-                else:
-                    sum_neighbours(a, product, K, h0_ps, h0)
-                if cb > 0:
+                sum_neighbours(a, product, first_terms, h0_ps)
+                if cb > 0 and a < quarters - 1:
                     head(head_ps, h2_before, a, second_half)
                     park(cb - 1, a, head_ps)
+                if cb > 0 and a == quarters - 1:
+                    head(head_ps, h2_before, a, third_quarter)
+                sum_neighbours(a, product, last_terms, h0_ps)
+                nc.scalar.activation(h0[:, a, :], h0_ps[:, a, :], RELU, bias=bias_cols[:, B0_ROW + a : B0_ROW + a + 1])
+            if cb > 0:
+                head(head_ps, h2_before, quarters - 1, fourth_quarter)
+                park(cb - 1, quarters - 1, head_ps)
             hidden_layer(h0, w1_sb, B1_ROW, h1)
             hidden_layer(h1, w2_sb, B2_ROW, h2)
             h2_before = h2

@@ -7,6 +7,7 @@ U16 = mybir.dt.uint16
 MULT = mybir.AluOpType.mult
 ADD = mybir.AluOpType.add
 RELU = mybir.ActivationFunctionType.Relu
+INNERMOST = mybir.AxisListType.X
 
 P = 128
 C, S, K = 512, 1024, 16
@@ -29,7 +30,7 @@ def tile_lcn_b_kernel(tc, x, w0, b0, w1, b1, w2, b2, fc_w, fc_b, offs, out):
         tc.tile_pool(name="held", bufs=1) as held,
         tc.tile_pool(name="products", bufs=4) as products,
         tc.tile_pool(name="layers", bufs=2) as layers,
-        tc.tile_pool(name="results", bufs=C // P * (M // BANK)) as results,
+        tc.tile_pool(name="results", bufs=C // P * (M // BANK) + 1) as results,
         tc.psum_pool(name="psum_sums", bufs=1) as psum_sums,
         tc.psum_pool(name="psum_hidden", bufs=5) as psum_hidden,
         tc.psum_pool(name="psum_wide", bufs=2) as psum_wide,
@@ -99,6 +100,14 @@ def tile_lcn_b_kernel(tc, x, w0, b0, w1, b1, w2, b2, fc_w, fc_b, offs, out):
                     stop=(k == K - 1),
                 )
 
+        def sum_on_vector(a, product, terms, h0_ps):
+            by_term = product[:].rearrange("p (d k) -> p d k", k=K)
+            sums = held.tile([P, P], F32, name="sums")
+            nc.vector.tensor_reduce(sums[:], by_term[:, :, terms.start : terms.stop], INNERMOST, ADD)
+            nc.tensor.matmul(
+                h0_ps[:, a, :], sums[:], identity[:], is_transpose=True, start=(terms.start == 0), stop=(terms.stop == K)
+            )
+
         def hidden_layer(h_in, w_sb, b_row, h_out):
             blocks_in, blocks_out = h_in.shape[1], h_out.shape[1]
             for g in range(blocks_out):
@@ -113,28 +122,29 @@ def tile_lcn_b_kernel(tc, x, w0, b0, w1, b1, w2, b2, fc_w, fc_b, offs, out):
                     )
                 nc.scalar.activation(h_out[:, g, :], hidden_ps[:], RELU, bias=bias_cols[:, b_row + g : b_row + g + 1])
 
-        def head(head_ps, h2, mc, blocks):
+        def head(head_ps, h2, first, blocks):
+            width = head_ps.shape[1]
             for f in blocks:
                 nc.tensor.matmul(
-                    head_ps[:],
+                    head_ps,
                     h2[:, f, :],
-                    fc_w_sb[mc][:, f, :],
+                    fc_w_sb[first // BANK][:, f, first % BANK : first % BANK + width],
                     start=(f == 0),
                     stop=(f == D2 // P - 1),
                 )
 
-        def add_bias_and_store(cb, mc, product_with_fc_w, result):
-            first = mc * BANK % PIECE
-            fc_b_part = fc_b_pieces[mc * BANK // PIECE][:, first : first + BANK]
-            nc.vector.tensor_tensor(result[:], product_with_fc_w[:], fc_b_part, ADD)
-            nc.sync.dma_start(out[cb * P : (cb + 1) * P, mc * BANK : (mc + 1) * BANK], result[:])
+        def add_bias_and_store(cb, first, product_with_fc_w, result):
+            width = result.shape[1]
+            fc_b_part = fc_b_pieces[first // PIECE][:, first % PIECE : first % PIECE + width]
+            nc.vector.tensor_tensor(result, product_with_fc_w, fc_b_part, ADD)
+            nc.sync.dma_start(out[cb * P : (cb + 1) * P, first : first + width], result)
 
         parked = []
 
-        def park(cb, mc, head_ps):
+        def park(cb, first, head_ps):
             result = results.tile([P, BANK], F32, name="result")
             nc.scalar.copy(result[:], head_ps[:])
-            parked.append((cb, mc, result))
+            parked.append((cb, first, result))
 
         quarters = M // BANK
         assert quarters == D0 // P
@@ -152,25 +162,29 @@ def tile_lcn_b_kernel(tc, x, w0, b0, w1, b1, w2, b2, fc_w, fc_b, offs, out):
                 product = look_up(cb, a)
                 if cb > 0:
                     head_ps = psum_wide.tile([P, BANK], F32, name="head_ps")
-                    head(head_ps, h2_before, a, first_half)
+                    head(head_ps[:], h2_before, a * BANK, first_half)
                 sum_neighbours(a, product, first_terms, h0_ps)
                 if cb > 0 and a < quarters - 1:
-                    head(head_ps, h2_before, a, second_half)
-                    park(cb - 1, a, head_ps)
+                    head(head_ps[:], h2_before, a * BANK, second_half)
+                    park(cb - 1, a * BANK, head_ps)
                 if cb > 0 and a == quarters - 1:
-                    head(head_ps, h2_before, a, third_quarter)
-                sum_neighbours(a, product, last_terms, h0_ps)
+                    head(head_ps[:], h2_before, a * BANK, third_quarter)
+                if cb == C // P - 1 and a == D0 // P - 1:
+                    sum_on_vector(a, product, last_terms, h0_ps)
+                else:
+                    sum_neighbours(a, product, last_terms, h0_ps)
                 nc.scalar.activation(h0[:, a, :], h0_ps[:, a, :], RELU, bias=bias_cols[:, B0_ROW + a : B0_ROW + a + 1])
             if cb > 0:
-                head(head_ps, h2_before, quarters - 1, fourth_quarter)
-                park(cb - 1, quarters - 1, head_ps)
+                head(head_ps[:], h2_before, (quarters - 1) * BANK, fourth_quarter)
+                park(cb - 1, (quarters - 1) * BANK, head_ps)
             hidden_layer(h0, w1_sb, B1_ROW, h1)
             hidden_layer(h1, w2_sb, B2_ROW, h2)
             h2_before = h2
-        for cb, mc, result in parked:
-            add_bias_and_store(cb, mc, result, result)
-        for mc in range(quarters):
+        for cb, first, result in parked:
+            add_bias_and_store(cb, first, result[:], result[:])
+        widths = [BANK] * (quarters - 1) + [BANK // 2] * 2
+        for i, width in enumerate(widths):
             head_ps = psum_wide.tile([P, BANK], F32, name="head_ps")
-            head(head_ps, h2_before, mc, all_blocks)
+            head(head_ps[:, 0:width], h2_before, sum(widths[:i]), all_blocks)
             result = results.tile([P, BANK], F32, name="result")
-            add_bias_and_store(C // P - 1, mc, head_ps, result)
+            add_bias_and_store(C // P - 1, sum(widths[:i]), head_ps[:, 0:width], result[:, 0:width])

@@ -150,7 +150,6 @@ def tile_lcn_b_kernel(tc, x, w0, b0, w1, b1, w2, b2, fc_w, fc_b, offs, out):
         assert quarters == D0 // P
         all_blocks = range(D2 // P)
         first_half, second_half = range(D2 // P // 2), range(D2 // P // 2, D2 // P)
-        third_quarter, fourth_quarter = range(D2 // P // 2, D2 // P * 3 // 4), range(D2 // P * 3 // 4, D2 // P)
         first_terms, last_terms = range(K // 2), range(K // 2, K)
         h2_before = None
         for cb in range(C // P):
@@ -158,6 +157,7 @@ def tile_lcn_b_kernel(tc, x, w0, b0, w1, b1, w2, b2, fc_w, fc_b, offs, out):
             h0 = layers.tile([P, D0 // P, P], BF16, name="h0")
             h1 = layers.tile([P, D1 // P, P], BF16, name="h1")
             h2 = layers.tile([P, D2 // P, P], BF16, name="h2")
+            kept_back = 2 if cb == C // P - 1 else 1
             for a in range(D0 // P):
                 product = look_up(cb, a)
                 if cb > 0:
@@ -168,14 +168,14 @@ def tile_lcn_b_kernel(tc, x, w0, b0, w1, b1, w2, b2, fc_w, fc_b, offs, out):
                     head(head_ps[:], h2_before, a * BANK, second_half)
                     park(cb - 1, a * BANK, head_ps)
                 if cb > 0 and a == quarters - 1:
-                    head(head_ps[:], h2_before, a * BANK, third_quarter)
+                    head(head_ps[:], h2_before, a * BANK, range(D2 // P // 2, D2 // P - kept_back))
                 if cb == C // P - 1 and a == D0 // P - 1:
                     sum_on_vector(a, product, last_terms, h0_ps)
                 else:
                     sum_neighbours(a, product, last_terms, h0_ps)
                 nc.scalar.activation(h0[:, a, :], h0_ps[:, a, :], RELU, bias=bias_cols[:, B0_ROW + a : B0_ROW + a + 1])
             if cb > 0:
-                head(head_ps[:], h2_before, (quarters - 1) * BANK, fourth_quarter)
+                head(head_ps[:], h2_before, (quarters - 1) * BANK, range(D2 // P - kept_back, D2 // P))
                 park(cb - 1, (quarters - 1) * BANK, head_ps)
             hidden_layer(h0, w1_sb, B1_ROW, h1)
             hidden_layer(h1, w2_sb, B2_ROW, h2)

import concourse.mybir as mybir
from concourse.masks import make_identity

F32 = mybir.dt.float32
BF16 = mybir.dt.bfloat16
U16 = mybir.dt.uint16
MULT = mybir.AluOpType.mult
ADD = mybir.AluOpType.add
RELU = mybir.ActivationFunctionType.Relu
INNERMOST = mybir.AxisListType.X

P = 128
C, S, K = 512, 1024, 16
D0, D1, D2, M = 512, 512, 1024, 2048
N = D0 * K
PIECE = S
BANK = 512

B0_ROW = 0
B1_ROW = B0_ROW + D0 // P
B2_ROW = B1_ROW + D1 // P
ROWS_USED = B2_ROW + D2 // P

FLOPS = 2 * C * (N + D0 * D1 + D1 * D2 + D2 * M)


def tile_lcn_b_kernel(tc, x, w0, b0, w1, b1, w2, b2, fc_w, fc_b, offs, out):
    nc = tc.nc
    with (
        tc.tile_pool(name="held", bufs=1) as held,
        tc.tile_pool(name="products", bufs=4) as products,
        tc.tile_pool(name="layers", bufs=2) as layers,
        tc.tile_pool(name="results", bufs=C // P * (M // BANK) + 1) as results,
        tc.psum_pool(name="psum_sums", bufs=1) as psum_sums,
        tc.psum_pool(name="psum_hidden", bufs=5) as psum_hidden,
        tc.psum_pool(name="psum_wide", bufs=2) as psum_wide,
    ):
        identity = held.tile([P, P], F32, name="identity")
        make_identity(nc, identity[:])

        offsets = held.tile([P, N // 16], U16, name="offsets")
        nc.sync.dma_start(offsets[:], offs)
        x_blocks = [held.tile([P, S], F32, name="x%d" % cb) for cb in range(C // P)]
        nc.scalar.dma_start(x_blocks[0][:], x[0:P, :])
        bias_rows = held.tile([P, P], F32, name="bias_rows")
        nc.vector.memset(bias_rows[:], 0.0)
        nc.scalar.dma_start(bias_rows[B0_ROW:B1_ROW, :], b0.rearrange("(a p) o -> a (p o)", p=P))
        nc.scalar.dma_start(bias_rows[B1_ROW:B2_ROW, :], b1.rearrange("(a p) o -> a (p o)", p=P))
        nc.scalar.dma_start(bias_rows[B2_ROW:ROWS_USED, :], b2.rearrange("(a p) o -> a (p o)", p=P))

        w0_row = w0.rearrange("o n -> (o n)")
        w0_pieces = [held.tile([P, PIECE], F32, name="w0_%d" % r) for r in range(N // PIECE)]
        for r in range(N // PIECE):
            nc.sync.dma_start(w0_pieces[r][:], w0_row[r * PIECE : (r + 1) * PIECE].partition_broadcast(P))
        nc.sync.dma_start(x_blocks[1][:], x[P : 2 * P, :])

        w1_sb = held.tile([P, D0 // P, D1], BF16, name="w1_sb")
        nc.sync.dma_start(w1_sb[:], w1.rearrange("(a p) e -> p a e", p=P))
        w2_sb = held.tile([P, D1 // P, D2], BF16, name="w2_sb")
        nc.sync.dma_start(w2_sb[:], w2.rearrange("(a p) f -> p a f", p=P))
        fc_w_blocks = fc_w.rearrange("(a p) m -> p a m", p=P)
        fc_w_sb = [held.tile([P, D2 // P, BANK], BF16, name="fc_w_%d" % mc) for mc in range(M // BANK)]
        for mc in range(M // BANK):
            nc.sync.dma_start(fc_w_sb[mc][:], fc_w_blocks[:, :, mc * BANK : (mc + 1) * BANK])
        for cb in range(2, C // P):
            nc.sync.dma_start(x_blocks[cb][:], x[cb * P : (cb + 1) * P, :])
        fc_b_row = fc_b.rearrange("m o -> (m o)")
        fc_b_pieces = []
        for i in range(M // PIECE):
            fc_b_piece = held.tile([P, PIECE], F32, name="fc_b_%d" % i, tag="w0_%d" % (N // PIECE - M // PIECE + i))
            nc.sync.dma_start(fc_b_piece[:], fc_b_row[i * PIECE : (i + 1) * PIECE].partition_broadcast(P))
            fc_b_pieces.append(fc_b_piece)

        bias_cols_ps = psum_wide.tile([P, BANK], F32, name="bias_cols_ps", tag="head_ps")
        nc.tensor.transpose(bias_cols_ps[:, 0:P], bias_rows[:], identity[:])
        bias_cols = held.tile([P, P], F32, name="bias_cols")
        nc.scalar.copy(bias_cols[:], bias_cols_ps[:, 0:P])

        def look_up(cb, a):
            product = products.tile([P, P * K], F32, name="product")
            for half in range(P * K // PIECE):
                r = a * (P * K // PIECE) + half
                nc.vector.tensor_tensor(
                    product[:, half * PIECE : (half + 1) * PIECE],
                    x_blocks[cb][:].indirect(offsets[:, r * (PIECE // 16) : (r + 1) * (PIECE // 16)]),
                    w0_pieces[r][:],
                    MULT,
                )
            return product

        def sum_neighbours(a, product, terms, h0_ps):
            by_term = product[:].rearrange("p (d k) -> p d k", k=K)
            for k in terms:
                nc.tensor.matmul(
                    h0_ps[:, a, :],
                    by_term[:, :, k],
                    identity[:],
                    is_transpose=True,
                    start=(k == 0),
                    stop=(k == K - 1),
                )

        def sum_on_vector(a, product, terms, h0_ps):
            by_term = product[:].rearrange("p (d k) -> p d k", k=K)
            sums = held.tile([P, P], F32, name="sums")
            nc.vector.tensor_reduce(sums[:], by_term[:, :, terms.start : terms.stop], INNERMOST, ADD)
            nc.tensor.matmul(
                h0_ps[:, a, :], sums[:], identity[:], is_transpose=True, start=(terms.start == 0), stop=(terms.stop == K)
            )

        def hidden_layer(h_in, w_sb, b_row, h_out):
            blocks_in, blocks_out = h_in.shape[1], h_out.shape[1]
            for g in range(blocks_out):
                hidden_ps = psum_hidden.tile([P, P], F32, name="hidden_ps")
                for a in range(blocks_in):
                    nc.tensor.matmul(
                        hidden_ps[:],
                        w_sb[:, a, g * P : (g + 1) * P],
                        h_in[:, a, :],
                        start=(a == 0),
                        stop=(a == blocks_in - 1),
                    )
                nc.scalar.activation(h_out[:, g, :], hidden_ps[:], RELU, bias=bias_cols[:, b_row + g : b_row + g + 1])

        def head(head_ps, h2, first, blocks):
            width = head_ps.shape[1]
            for f in blocks:
                nc.tensor.matmul(
                    head_ps,
                    h2[:, f, :],
                    fc_w_sb[first // BANK][:, f, first % BANK : first % BANK + width],
                    start=(f == 0),
                    stop=(f == D2 // P - 1),
                )

        def add_bias_and_store(cb, first, product_with_fc_w, result):
            width = result.shape[1]
            fc_b_part = fc_b_pieces[first // PIECE][:, first % PIECE : first % PIECE + width]
            nc.vector.tensor_tensor(result, product_with_fc_w, fc_b_part, ADD)
            nc.sync.dma_start(out[cb * P : (cb + 1) * P, first : first + width], result)

        parked = []

        def park(cb, first, head_ps):
            result = results.tile([P, BANK], F32, name="result")
            nc.scalar.copy(result[:], head_ps[:])
            parked.append((cb, first, result))

        quarters = M // BANK
        assert quarters == D0 // P
        all_blocks = range(D2 // P)
        first_half, second_half = range(D2 // P // 2), range(D2 // P // 2, D2 // P)
        first_terms, last_terms = range(K // 2), range(K // 2, K)
        h2_before = None
        for cb in range(C // P):
            h0_ps = psum_sums.tile([P, D0 // P, P], F32, name="h0_ps")
            h0 = layers.tile([P, D0 // P, P], BF16, name="h0")
            h1 = layers.tile([P, D1 // P, P], BF16, name="h1")
            h2 = layers.tile([P, D2 // P, P], BF16, name="h2")
            kept_back = 2 if cb == C // P - 1 else 1
            for a in range(D0 // P):
                product = look_up(cb, a)
                if cb > 0:
                    head_ps = psum_wide.tile([P, BANK], F32, name="head_ps")
                    head(head_ps[:], h2_before, a * BANK, first_half)
                sum_neighbours(a, product, first_terms, h0_ps)
                if cb > 0 and a < quarters - 1:
                    head(head_ps[:], h2_before, a * BANK, second_half)
                    park(cb - 1, a * BANK, head_ps)
                if cb > 0 and a == quarters - 1:
                    head(head_ps[:], h2_before, a * BANK, range(D2 // P // 2, D2 // P - kept_back))
                if cb == C // P - 1 and a == D0 // P - 1:
                    sum_on_vector(a, product, last_terms, h0_ps)
                else:
                    sum_neighbours(a, product, last_terms, h0_ps)
                nc.scalar.activation(h0[:, a, :], h0_ps[:, a, :], RELU, bias=bias_cols[:, B0_ROW + a : B0_ROW + a + 1])
            if cb > 0:
                head(head_ps[:], h2_before, (quarters - 1) * BANK, range(D2 // P - kept_back, D2 // P))
                park(cb - 1, (quarters - 1) * BANK, head_ps)
            hidden_layer(h0, w1_sb, B1_ROW, h1)
            hidden_layer(h1, w2_sb, B2_ROW, h2)
            h2_before = h2
        for cb, first, result in parked:
            add_bias_and_store(cb, first, result[:], result[:])
        widths = [BANK] * (quarters - 1) + [BANK // 2] * 2
        for i, width in enumerate(widths):
            head_ps = psum_wide.tile([P, BANK], F32, name="head_ps")
            head(head_ps[:, 0:width], h2_before, sum(widths[:i]), all_blocks)
            result = results.tile([P, BANK], F32, name="result")
            add_bias_and_store(C // P - 1, sum(widths[:i]), head_ps[:, 0:width], result[:, 0:width])
